import numpy as np
import ml_dtypes


def mxq(x, axis, fmt="e4m3"):
    dtype, down = {"e4m3": (ml_dtypes.float8_e4m3fn, 7), "e5m2": (ml_dtypes.float8_e5m2, 14)}[fmt]
    v = np.moveaxis(np.asarray(x, np.float32).astype(ml_dtypes.bfloat16).astype(np.float64), axis, -1)
    blocks = v.reshape(v.shape[:-1] + (-1, 32))
    amax = np.abs(blocks).max(-1, keepdims=True)
    byte = np.maximum(np.where(amax > 0, np.frexp(amax)[1] - 1 + 127, 0) - down, 1)
    scale = np.exp2(byte - 127.0)
    codes = (blocks / scale).astype(np.float32).astype(dtype).astype(np.float64)
    return np.moveaxis((codes * scale).reshape(v.shape), -1, axis)


WIDE = False


def mx_kscale(k):
    if not WIDE:
        return np.ones(k)
    levels = np.array([10, -10, 5, -5, 0])
    a = np.random.permutation(np.resize(levels, k // 512 * 4)).reshape(k // 512, 4)
    idx = np.arange(k)
    return np.exp2(a[idx // 512, idx % 128 // 32])


BF16 = ml_dtypes.bfloat16


def bf(x):
    return np.asarray(x, np.float32).astype(BF16)


def f64(x):
    return np.asarray(x).astype(np.float64)


E2M1 = np.array([0.0, 0.5, 1.0, 1.5, 2.0, 3.0, 4.0, 6.0, -0.0, -0.5, -1.0, -1.5, -2.0, -3.0, -4.0, -6.0])


def pack_weight(w, fmt):
    k, n = w.shape
    w = f64(bf(w)).reshape(k // 32, 32, n)
    amax = np.abs(w).max(1)
    if fmt == "e4m3":
        byte = np.frexp(amax)[1] - 1 + 127 - 7
    else:
        mant, ex = np.frexp(amax / 6.0)
        byte = np.where(mant > 0.5, ex, ex - 1) + 127
    byte = np.clip(np.where(amax > 0, byte, 1), 1, 254)
    scaled = (w * np.exp2(127.0 - byte)[:, None, :]).reshape(k, n).astype(np.float32)
    by_word = np.ascontiguousarray(scaled.reshape(k // 512, 128, 4, n).transpose(0, 1, 3, 2))
    if fmt == "e4m3":
        words = by_word.astype(ml_dtypes.float8_e4m3fn).view(np.uint8)
    else:
        c = by_word.astype(ml_dtypes.float4_e2m1fn).view(np.uint8) & 0xF
        words = c[..., 0::2] | (c[..., 1::2] << 4)
    return np.ascontiguousarray(words), np.ascontiguousarray(byte.astype(np.uint8).reshape(k // 512, 16, n))


def unpack_weight(words, scales, fmt):
    g, p, n, _ = words.shape
    if fmt == "e4m3":
        vals = np.ascontiguousarray(words).view(ml_dtypes.float8_e4m3fn).astype(np.float64)
    else:
        nib = np.empty((g, p, n, 4), np.uint8)
        nib[..., 0::2] = words & 0xF
        nib[..., 1::2] = words >> 4
        vals = E2M1[nib]
    vals = vals * np.repeat(np.exp2(scales.astype(np.float64) - 127.0), 8, axis=1)[..., None]
    return vals.transpose(0, 1, 3, 2).reshape(g * 512, n)

def pack4(w):
    words, scales = pack_weight(w, "e2m1")
    return words.reshape(words.shape[0], 128, -1), scales


def unpack4(words, scales):
    return unpack_weight(words.reshape(words.shape[0], 128, -1, 2), scales, "e2m1")


B, D = 4096, 512


def softplus(v):
    return np.logaddexp(v, 0.0)


def setup_inputs():
    s = mx_kscale(D)
    xt = bf(np.random.standard_normal((B, D)) * 1.3 * s)
    eps = bf(np.random.standard_normal((B, D)))
    x = bf(np.random.standard_normal((B, D)))
    t_rand = bf(np.random.uniform(0.0, 1.0, (B, 1)))
    Wm_words, Wm_scales = pack4((np.random.standard_normal((D, D)) / np.sqrt(D) / s[None, :]).T)
    bm = bf(np.random.standard_normal(D) * 0.5)
    Wv_words, Wv_scales = pack4((np.random.standard_normal((D, D)) / np.sqrt(D) / s[None, :]).T)
    bv = bf(np.random.standard_normal(D) * 0.5)
    return {"xt": xt, "eps": eps, "x": x, "t_rand": t_rand,
            "Wm_words": Wm_words, "Wm_scales": Wm_scales, "bm": bm,
            "Wv_words": Wv_words, "Wv_scales": Wv_scales, "bv": bv}


def reference(xt, eps, x, t_rand, Wm_words, Wm_scales, bm, Wv_words, Wv_scales, bv):
    xq = mxq(f64(xt), 1, "e4m3")
    mu = (xq @ unpack4(Wm_words, Wm_scales)) + f64(bm)
    sigma = softplus((xq @ unpack4(Wv_words, Wv_scales)) + f64(bv))
    x_prime = mu + sigma * f64(eps)
    return (1.0 - f64(t_rand)) * f64(x) + f64(t_rand) * x_prime

@@ -1,0 +1,184 @@
+from contextlib import ExitStack
+
+import concourse.mybir as mybir
+from concourse.masks import make_identity
+
+F32 = mybir.dt.float32
+BF16 = mybir.dt.bfloat16
+I32 = mybir.dt.int32
+U32 = mybir.dt.uint32
+U8 = mybir.dt.uint8
+FP8X4 = mybir.dt.float8_e4m3fn_x4
+FP4X4 = mybir.dt.float4_e2m1fn_x4
+ALU = mybir.AluOpType
+ACT = mybir.ActivationFunctionType
+
+P = 128
+ROWS = 4096
+D = 512
+TILES = ROWS // P
+QUAD = 4
+QUADS = TILES // QUAD
+LOAD = 8
+TINY = 2.0 ** -63
+
+FLOPS = 2 * 2 * ROWS * D * D
+
+
+def load_fp4_weight(nc, pool, words, scales, name):
+    w_words = pool.tile([P, 2 * D], U8, name=name + "_words", align_bytes=64)
+    nc.sync.dma_start(out=w_words[:].bitcast(I32), in_=words[0].bitcast(I32))
+    w_plane = pool.tile([P, D], U8, name=name + "_plane", align_bytes=64)
+    nc.vector.memset(w_plane[:].bitcast(I32), 0)
+    for quadrant in range(4):
+        nc.sync.dma_start(
+            out=w_plane[32 * quadrant : 32 * quadrant + 4, :].bitcast(I32),
+            in_=scales[0, 4 * quadrant : 4 * quadrant + 4, :].bitcast(I32),
+        )
+    return w_words, w_plane
+
+
+def tile_diffscm_pb_t_kernel(
+    tc, xt, eps, x, t_rand, Wm_words, Wm_scales, bm, Wv_words, Wv_scales, bv, out
+):
+    nc = tc.nc
+    xt_rows = xt.rearrange("(p i) k -> p i k", i=TILES)
+    eps_rows = eps.rearrange("(p i) n -> p i n", i=TILES)
+    x_rows = x.rearrange("(p i) n -> p i n", i=TILES)
+    out_rows = out.rearrange("(p i) n -> p i n", i=TILES)
+
+    with ExitStack() as ctx:
+        keep = ctx.enter_context(tc.tile_pool(name="keep", bufs=1))
+        stage = ctx.enter_context(tc.tile_pool(name="stage", bufs=2))
+        flow = ctx.enter_context(tc.tile_pool(name="flow", bufs=3))
+        ctx.enter_context(tc.manual_schedule())
+        psum_t = ctx.enter_context(tc.psum_pool(name="psum_t", bufs=2))
+        psum_mm = ctx.enter_context(tc.psum_pool(name="psum_mm", bufs=3))
+
+        xt_sb = keep.tile([P, TILES, D], BF16, name="xt_sb")
+        eps_sb = keep.tile([P, TILES, D], BF16, name="eps_sb")
+        x_sb = keep.tile([P, TILES, D], BF16, name="x_sb")
+        nc.sync.dma_start(out=xt_sb[:, 0:QUAD, :], in_=xt_rows[:, 0:QUAD, :])
+        wv_words, wv_plane = load_fp4_weight(nc, keep, Wv_words, Wv_scales, "wv")
+        wm_words, wm_plane = load_fp4_weight(nc, keep, Wm_words, Wm_scales, "wm")
+        t_bf = keep.tile([P, TILES], BF16, name="t_bf")
+        nc.sync.dma_start(out=t_bf[:], in_=t_rand.rearrange("(p i) o -> p (i o)", i=TILES))
+        bv_all = keep.tile([P, D], BF16, name="bv_all")
+        nc.sync.dma_start(out=bv_all[:], in_=bv.partition_broadcast(P))
+        bm_all = keep.tile([P, D], BF16, name="bm_all")
+        nc.sync.dma_start(out=bm_all[:], in_=bm.partition_broadcast(P))
+        nc.sync.dma_start(out=xt_sb[:, QUAD:LOAD, :], in_=xt_rows[:, QUAD:LOAD, :])
+        for b in range(TILES // LOAD):
+            rows = slice(b * LOAD, (b + 1) * LOAD)
+            if b > 0:
+                nc.sync.dma_start(out=xt_sb[:, rows, :], in_=xt_rows[:, rows, :])
+            nc.sync.dma_start(out=x_sb[:, rows, :], in_=x_rows[:, rows, :])
+            nc.sync.dma_start(out=eps_sb[:, rows, :], in_=eps_rows[:, rows, :])
+
+        ident = keep.tile([P, P], F32, name="ident")
+        make_identity(nc, ident[:])
+        t_f32 = keep.tile([P, TILES], F32, name="t_f32")
+        nc.vector.tensor_copy(out=t_f32[:], in_=t_bf[:])
+        one_minus_t = keep.tile([P, TILES], F32, name="one_minus_t")
+        nc.vector.tensor_scalar(
+            out=one_minus_t[:], in0=t_bf[:], scalar1=-1.0, scalar2=1.0, op0=ALU.mult, op1=ALU.add
+        )
+
+        grouped_of = {}
+        codes_of = {}
+        u_of = {}
+        s_of = {}
+        mu_of = {}
+        kept_of = {}
+
+        def turn(k):
+            grouped = stage.tile([P, QUAD * P * 4], BF16, name="grouped", align_bytes=64)
+            grouped_words = grouped[:].bitcast(F32).rearrange("p (i r h) -> p i r h", i=QUAD, r=P, h=2)
+            for pair in range(QUAD // 2):
+                turned = psum_t.tile([P, 2, 2, P], F32, name="turned")
+                for i in range(2):
+                    words = xt_sb[:, k * QUAD + 2 * pair + i, :].bitcast(F32)
+                    for h in range(2):
+                        nc.tensor.transpose(turned[:, i, h, :], words[:, h : D // 2 : 2], ident[:])
+                nc.scalar.copy(
+                    out=grouped_words[:, 2 * pair : 2 * pair + 2, :, :],
+                    in_=turned[:].rearrange("p i h r -> p i r h"),
+                )
+            grouped_of[k] = grouped
+
+        def quantise(k):
+            codes = stage.tile([P, QUAD * P], U32, name="codes", align_bytes=64)
+            planes = stage.tile([P, QUAD * P], U8, name="planes", align_bytes=64)
+            nc.vector.quantize_mx(out=codes[:].bitcast(FP8X4), scales=planes[:], in_=grouped_of[k][:])
+            codes_of[k] = (codes, planes)
+
+        def head(acc, k, i, w_words, w_plane):
+            codes, planes = codes_of[k]
+            cols = slice(i * P, (i + 1) * P)
+            nc.tensor.matmul_mx(
+                out=acc[:],
+                lhsT=codes[:, cols].bitcast(FP8X4),
+                lhsT_scale=planes[:, cols],
+                rhs=w_words[:].bitcast(FP4X4),
+                rhs_scale=w_plane[:],
+                start=True,
+                stop=True,
+            )
+
+        def heads(k):
+            u_of[k] = flow.tile([P, QUAD, D], F32, name="u", bufs=4)
+            s_of[k] = flow.tile([P, QUAD, D], F32, name="s")
+            mu_of[k] = flow.tile([P, QUAD, D], F32, name="mu")
+            for i in range(QUAD):
+                acc_v = psum_mm.tile([P, D], F32, name="acc_v")
+                head(acc_v, k, i, wv_words, wv_plane)
+                nc.vector.tensor_tensor(out=u_of[k][:, i, :], in0=acc_v[:], in1=bv_all[:], op=ALU.add)
+                acc_m = psum_mm.tile([P, D], F32, name="acc_m")
+                head(acc_m, k, i, wm_words, wm_plane)
+                nc.vector.tensor_tensor(out=mu_of[k][:, i, :], in0=acc_m[:], in1=bm_all[:], op=ALU.add)
+                nc.scalar.activation(out=s_of[k][:, i, :], in_=u_of[k][:, i, :], func=ACT.Sigmoid, scale=-1.0)
+
+        def keep_share(k):
+            kept_of[k] = flow.tile([P, QUAD, D], F32, name="kept", bufs=2)
+            for i in range(QUAD):
+                row = k * QUAD + i
+                nc.scalar.activation(
+                    out=kept_of[k][:, i, :], in_=x_sb[:, row, :], func=ACT.Copy, scale=one_minus_t[:, row : row + 1]
+                )
+
+        def log(k):
+            flat = s_of[k][:].rearrange("p i n -> p (i n)")
+            nc.scalar.activation(out=flat, in_=flat, func=ACT.Ln, bias=TINY)
+
+        def blend(k):
+            u, s, mu, kept = u_of[k], s_of[k], mu_of[k], kept_of[k]
+            for i in range(QUAD):
+                nc.vector.scalar_tensor_tensor(
+                    out=s[:, i, :], in0=s[:, i, :], scalar=-1.0, in1=u[:, i, :], op0=ALU.mult, op1=ALU.max
+                )
+                nc.gpsimd.tensor_tensor(out=s[:, i, :], in0=s[:, i, :], in1=eps_sb[:, k * QUAD + i, :], op=ALU.mult)
+            for i in range(QUAD):
+                row = k * QUAD + i
+                nc.vector.tensor_tensor(out=mu[:, i, :], in0=mu[:, i, :], in1=s[:, i, :], op=ALU.add)
+                nc.vector.scalar_tensor_tensor(
+                    out=u[:, i, :], in0=mu[:, i, :], scalar=t_f32[:, row : row + 1], in1=kept[:, i, :],
+                    op0=ALU.mult, op1=ALU.add,
+                )
+            nc.sync.dma_start(out=out_rows[:, k * QUAD : (k + 1) * QUAD, :], in_=u[:])
+
+        turn(0)
+        quantise(0)
+        for step in range(QUADS + 2):
+            if step + 1 < QUADS:
+                turn(step + 1)
+            if step < QUADS:
+                heads(step)
+            if step + 1 < QUADS:
+                quantise(step + 1)
+            if step >= 2:
+                keep_share(step - 2)
+            if step < QUADS and step % 2 == 1:
+                log(step - 1)
+                log(step)
+            if step >= 2:
+                blend(step - 2)

@@ -156,7 +156,7 @@ def tile_diffscm_pb_t_kernel(
                 nc.vector.scalar_tensor_tensor(
                     out=s[:, i, :], in0=s[:, i, :], scalar=-1.0, in1=u[:, i, :], op0=ALU.mult, op1=ALU.max
                 )
-                nc.gpsimd.tensor_tensor(out=s[:, i, :], in0=s[:, i, :], in1=eps_sb[:, k * QUAD + i, :], op=ALU.mult)
+                nc.vector.tensor_tensor(out=s[:, i, :], in0=s[:, i, :], in1=eps_sb[:, k * QUAD + i, :], op=ALU.mult)
             for i in range(QUAD):
                 row = k * QUAD + i
                 nc.vector.tensor_tensor(out=mu[:, i, :], in0=mu[:, i, :], in1=s[:, i, :], op=ALU.add)

@@ -150,16 +150,21 @@ def tile_diffscm_pb_t_kernel(
             flat = s_of[k][:].rearrange("p i n -> p (i n)")
             nc.scalar.activation(out=flat, in_=flat, func=ACT.Ln, bias=TINY)
 
-        def blend(k):
-            u, s, mu, kept = u_of[k], s_of[k], mu_of[k], kept_of[k]
+        def spread(k, product_engine):
+            u, s = u_of[k], s_of[k]
             for i in range(QUAD):
                 nc.vector.scalar_tensor_tensor(
                     out=s[:, i, :], in0=s[:, i, :], scalar=-1.0, in1=u[:, i, :], op0=ALU.mult, op1=ALU.max
                 )
-                nc.vector.tensor_tensor(out=s[:, i, :], in0=s[:, i, :], in1=eps_sb[:, k * QUAD + i, :], op=ALU.mult)
+            for i in range(QUAD):
+                product_engine.tensor_tensor(out=s[:, i, :], in0=s[:, i, :], in1=eps_sb[:, k * QUAD + i, :], op=ALU.mult)
+
+        def blend(k):
+            u, s, mu, kept = u_of[k], s_of[k], mu_of[k], kept_of[k]
+            for i in range(QUAD):
+                nc.vector.tensor_tensor(out=mu[:, i, :], in0=mu[:, i, :], in1=s[:, i, :], op=ALU.add)
             for i in range(QUAD):
                 row = k * QUAD + i
-                nc.vector.tensor_tensor(out=mu[:, i, :], in0=mu[:, i, :], in1=s[:, i, :], op=ALU.add)
                 nc.vector.scalar_tensor_tensor(
                     out=u[:, i, :], in0=mu[:, i, :], scalar=t_f32[:, row : row + 1], in1=kept[:, i, :],
                     op0=ALU.mult, op1=ALU.add,
@@ -171,12 +176,13 @@ def tile_diffscm_pb_t_kernel(
         for step in range(QUADS + 2):
             if step + 1 < QUADS:
                 turn(step + 1)
+            if step >= 2:
+                keep_share(step - 2)
+                spread(step - 2, nc.gpsimd if step < QUADS else nc.vector)
             if step < QUADS:
                 heads(step)
             if step + 1 < QUADS:
                 quantise(step + 1)
-            if step >= 2:
-                keep_share(step - 2)
             if step < QUADS and step % 2 == 1:
                 log(step - 1)
                 log(step)

@@ -19,7 +19,10 @@ D = 512
 TILES = ROWS // P
 QUAD = 4
 QUADS = TILES // QUAD
+BLOCKS = D // P
 LOAD = 8
+GATE_AHEAD = 3
+TURN_AHEAD = 4
 TINY = 2.0 ** -63
 
 FLOPS = 2 * 2 * ROWS * D * D
@@ -49,142 +52,171 @@ def tile_diffscm_pb_t_kernel(
 
     with ExitStack() as ctx:
         keep = ctx.enter_context(tc.tile_pool(name="keep", bufs=1))
-        stage = ctx.enter_context(tc.tile_pool(name="stage", bufs=2))
-        flow = ctx.enter_context(tc.tile_pool(name="flow", bufs=3))
+        flow = ctx.enter_context(tc.tile_pool(name="flow", bufs=2))
+        psum = ctx.enter_context(tc.psum_pool(name="psum", bufs=1))
         ctx.enter_context(tc.manual_schedule())
-        psum_t = ctx.enter_context(tc.psum_pool(name="psum_t", bufs=2))
-        psum_mm = ctx.enter_context(tc.psum_pool(name="psum_mm", bufs=3))
 
         xt_sb = keep.tile([P, TILES, D], BF16, name="xt_sb")
         eps_sb = keep.tile([P, TILES, D], BF16, name="eps_sb")
         x_sb = keep.tile([P, TILES, D], BF16, name="x_sb")
         nc.sync.dma_start(out=xt_sb[:, 0:QUAD, :], in_=xt_rows[:, 0:QUAD, :])
         wv_words, wv_plane = load_fp4_weight(nc, keep, Wv_words, Wv_scales, "wv")
+        bias_rows = keep.tile([P, P], BF16, name="bias_rows")
+        nc.vector.memset(bias_rows[:], 0.0)
+        nc.sync.dma_start(out=bias_rows[0:BLOCKS, :], in_=bv.rearrange("(j p) -> j p", p=P))
+        nc.sync.dma_start(out=bias_rows[BLOCKS : 2 * BLOCKS, :], in_=bm.rearrange("(j p) -> j p", p=P))
+        nc.sync.dma_start(out=xt_sb[:, QUAD:LOAD, :], in_=xt_rows[:, QUAD:LOAD, :])
         wm_words, wm_plane = load_fp4_weight(nc, keep, Wm_words, Wm_scales, "wm")
         t_bf = keep.tile([P, TILES], BF16, name="t_bf")
         nc.sync.dma_start(out=t_bf[:], in_=t_rand.rearrange("(p i) o -> p (i o)", i=TILES))
-        bv_all = keep.tile([P, D], BF16, name="bv_all")
-        nc.sync.dma_start(out=bv_all[:], in_=bv.partition_broadcast(P))
-        bm_all = keep.tile([P, D], BF16, name="bm_all")
-        nc.sync.dma_start(out=bm_all[:], in_=bm.partition_broadcast(P))
-        nc.sync.dma_start(out=xt_sb[:, QUAD:LOAD, :], in_=xt_rows[:, QUAD:LOAD, :])
         for b in range(TILES // LOAD):
             rows = slice(b * LOAD, (b + 1) * LOAD)
-            if b > 0:
-                nc.sync.dma_start(out=xt_sb[:, rows, :], in_=xt_rows[:, rows, :])
-            nc.sync.dma_start(out=x_sb[:, rows, :], in_=x_rows[:, rows, :])
+            if b + 1 < TILES // LOAD:
+                later = slice((b + 1) * LOAD, (b + 2) * LOAD)
+                nc.sync.dma_start(out=xt_sb[:, later, :], in_=xt_rows[:, later, :])
             nc.sync.dma_start(out=eps_sb[:, rows, :], in_=eps_rows[:, rows, :])
+            nc.sync.dma_start(out=x_sb[:, rows, :], in_=x_rows[:, rows, :])
 
         ident = keep.tile([P, P], F32, name="ident")
         make_identity(nc, ident[:])
+        ident_bf = keep.tile([P, P], BF16, name="ident_bf")
+        make_identity(nc, ident_bf[:])
         t_f32 = keep.tile([P, TILES], F32, name="t_f32")
-        nc.vector.tensor_copy(out=t_f32[:], in_=t_bf[:])
         one_minus_t = keep.tile([P, TILES], F32, name="one_minus_t")
-        nc.vector.tensor_scalar(
-            out=one_minus_t[:], in0=t_bf[:], scalar1=-1.0, scalar2=1.0, op0=ALU.mult, op1=ALU.add
-        )
-
+        bv_cols = keep.tile([P, BLOCKS], F32, name="bv_cols")
+        bm_cols = keep.tile([P, BLOCKS], F32, name="bm_cols")
         grouped_of = {}
+        turned_of = {}
         codes_of = {}
-        u_of = {}
-        s_of = {}
-        mu_of = {}
+        spread_of = {}
         kept_of = {}
+        done_of = {}
 
-        def turn(k):
-            grouped = stage.tile([P, QUAD * P * 4], BF16, name="grouped", align_bytes=64)
-            grouped_words = grouped[:].bitcast(F32).rearrange("p (i r h) -> p i r h", i=QUAD, r=P, h=2)
-            for pair in range(QUAD // 2):
-                turned = psum_t.tile([P, 2, 2, P], F32, name="turned")
-                for i in range(2):
-                    words = xt_sb[:, k * QUAD + 2 * pair + i, :].bitcast(F32)
-                    for h in range(2):
-                        nc.tensor.transpose(turned[:, i, h, :], words[:, h : D // 2 : 2], ident[:])
+        def turn(k, i):
+            if i == 0:
+                grouped_of[k] = flow.tile([P, QUAD * P * 4], BF16, name="grouped", align_bytes=64)
+            if i % 2 == 0:
+                turned_of[k] = psum.tile([P, 2, 2, P], F32, name="turned", tag="for_scalar", bufs=2)
+            words = xt_sb[:, k * QUAD + i, :].bitcast(F32)
+            for h in range(2):
+                nc.tensor.transpose(turned_of[k][:, i % 2, h, :], words[:, h : D // 2 : 2], ident[:])
+            if i % 2 == 1:
+                grouped_words = grouped_of[k][:].bitcast(F32).rearrange("p (i r h) -> p i r h", i=QUAD, r=P, h=2)
                 nc.scalar.copy(
-                    out=grouped_words[:, 2 * pair : 2 * pair + 2, :, :],
-                    in_=turned[:].rearrange("p i h r -> p i r h"),
+                    out=grouped_words[:, i - 1 : i + 1, :, :],
+                    in_=turned_of[k][:].rearrange("p i h r -> p i r h"),
                 )
-            grouped_of[k] = grouped
 
         def quantise(k):
-            codes = stage.tile([P, QUAD * P], U32, name="codes", align_bytes=64)
-            planes = stage.tile([P, QUAD * P], U8, name="planes", align_bytes=64)
+            codes = flow.tile([P, QUAD * P], U32, name="codes", bufs=5, align_bytes=64)
+            planes = flow.tile([P, QUAD * P], U8, name="planes", bufs=5, align_bytes=64)
             nc.vector.quantize_mx(out=codes[:].bitcast(FP8X4), scales=planes[:], in_=grouped_of[k][:])
             codes_of[k] = (codes, planes)
 
-        def head(acc, k, i, w_words, w_plane):
+        def head(acc, w_words, w_plane, j, k):
             codes, planes = codes_of[k]
-            cols = slice(i * P, (i + 1) * P)
             nc.tensor.matmul_mx(
                 out=acc[:],
-                lhsT=codes[:, cols].bitcast(FP8X4),
-                lhsT_scale=planes[:, cols],
-                rhs=w_words[:].bitcast(FP4X4),
-                rhs_scale=w_plane[:],
+                lhsT=w_words[:, 2 * P * j : 2 * P * (j + 1)].bitcast(FP4X4),
+                lhsT_scale=w_plane[:, P * j : P * (j + 1)],
+                rhs=codes[:].bitcast(FP8X4),
+                rhs_scale=planes[:],
                 start=True,
                 stop=True,
             )
 
-        def heads(k):
-            u_of[k] = flow.tile([P, QUAD, D], F32, name="u", bufs=4)
-            s_of[k] = flow.tile([P, QUAD, D], F32, name="s")
-            mu_of[k] = flow.tile([P, QUAD, D], F32, name="mu")
-            for i in range(QUAD):
-                acc_v = psum_mm.tile([P, D], F32, name="acc_v")
-                head(acc_v, k, i, wv_words, wv_plane)
-                nc.vector.tensor_tensor(out=u_of[k][:, i, :], in0=acc_v[:], in1=bv_all[:], op=ALU.add)
-                acc_m = psum_mm.tile([P, D], F32, name="acc_m")
-                head(acc_m, k, i, wm_words, wm_plane)
-                nc.vector.tensor_tensor(out=mu_of[k][:, i, :], in0=acc_m[:], in1=bm_all[:], op=ALU.add)
-                nc.scalar.activation(out=s_of[k][:, i, :], in_=u_of[k][:, i, :], func=ACT.Sigmoid, scale=-1.0)
-
-        def keep_share(k):
-            kept_of[k] = flow.tile([P, QUAD, D], F32, name="kept", bufs=2)
-            for i in range(QUAD):
-                row = k * QUAD + i
-                nc.scalar.activation(
-                    out=kept_of[k][:, i, :], in_=x_sb[:, row, :], func=ACT.Copy, scale=one_minus_t[:, row : row + 1]
-                )
+        def gate(k, j):
+            if j == 0:
+                spread_of[k] = flow.tile([P, BLOCKS, QUAD * P], F32, name="spread", bufs=4)
+            acc = psum.tile([P, QUAD * P], F32, name="acc_gate", tag="for_scalar", bufs=2)
+            head(acc, wv_words, wv_plane, j, k)
+            nc.scalar.activation(
+                out=spread_of[k][:, j, :], in_=acc[:], func=ACT.Sigmoid, bias=bv_cols[:, j : j + 1]
+            )
 
         def log(k):
-            flat = s_of[k][:].rearrange("p i n -> p (i n)")
+            flat = spread_of[k][:].rearrange("p j r -> p (j r)")
             nc.scalar.activation(out=flat, in_=flat, func=ACT.Ln, bias=TINY)
 
-        def spread(k, product_engine):
-            u, s = u_of[k], s_of[k]
-            for i in range(QUAD):
-                nc.vector.scalar_tensor_tensor(
-                    out=s[:, i, :], in0=s[:, i, :], scalar=-1.0, in1=u[:, i, :], op0=ALU.mult, op1=ALU.max
-                )
-            for i in range(QUAD):
-                product_engine.tensor_tensor(out=s[:, i, :], in0=s[:, i, :], in1=eps_sb[:, k * QUAD + i, :], op=ALU.mult)
+        def clamp(k, j):
+            acc = psum.tile([P, QUAD * P], F32, name="acc_clamp", tag="for_vector", bufs=6)
+            head(acc, wv_words, wv_plane, j, k)
+            part = spread_of[k][:, j, :]
+            nc.vector.scalar_tensor_tensor(
+                out=part, in0=acc[:], scalar=bv_cols[:, j : j + 1], in1=part, op0=ALU.add, op1=ALU.subtract
+            )
 
-        def blend(k):
-            u, s, mu, kept = u_of[k], s_of[k], mu_of[k], kept_of[k]
+        def noise(k, j):
+            eps_t = psum.tile([P, QUAD * P], BF16, name="eps_t", tag="for_vector", bufs=6)
             for i in range(QUAD):
-                nc.vector.tensor_tensor(out=mu[:, i, :], in0=mu[:, i, :], in1=s[:, i, :], op=ALU.add)
+                nc.tensor.transpose(
+                    eps_t[:, i * P : (i + 1) * P], eps_sb[:, k * QUAD + i, j * P : (j + 1) * P], ident_bf[:]
+                )
+            part = spread_of[k][:, j, :]
+            nc.vector.scalar_tensor_tensor(out=part, in0=part, scalar=0.0, in1=eps_t[:], op0=ALU.max, op1=ALU.mult)
+
+        def sample(k, j):
+            acc = psum.tile([P, QUAD * P], F32, name="acc_mean", tag="for_vector", bufs=6)
+            head(acc, wm_words, wm_plane, j, k)
+            part = spread_of[k][:, j, :]
+            nc.vector.scalar_tensor_tensor(
+                out=part, in0=acc[:], scalar=bm_cols[:, j : j + 1], in1=part, op0=ALU.add, op1=ALU.add
+            )
+
+        def keep_share(k):
+            kept_of[k] = flow.tile([P, QUAD, D], F32, name="kept")
             for i in range(QUAD):
                 row = k * QUAD + i
-                nc.vector.scalar_tensor_tensor(
-                    out=u[:, i, :], in0=mu[:, i, :], scalar=t_f32[:, row : row + 1], in1=kept[:, i, :],
+                nc.gpsimd.tensor_scalar(
+                    out=kept_of[k][:, i, :], in0=x_sb[:, row, :], scalar1=one_minus_t[:, row : row + 1], scalar2=0.0,
                     op0=ALU.mult, op1=ALU.add,
                 )
-            nc.sync.dma_start(out=out_rows[:, k * QUAD : (k + 1) * QUAD, :], in_=u[:])
 
-        turn(0)
-        quantise(0)
-        for step in range(QUADS + 2):
-            if step + 1 < QUADS:
-                turn(step + 1)
-            if step >= 2:
-                keep_share(step - 2)
-                spread(step - 2, nc.gpsimd if step < QUADS else nc.vector)
-            if step < QUADS:
-                heads(step)
-            if step + 1 < QUADS:
-                quantise(step + 1)
-            if step < QUADS and step % 2 == 1:
-                log(step - 1)
-                log(step)
-            if step >= 2:
-                blend(step - 2)
+        def blend(k, i):
+            if i == 0:
+                done_of[k] = flow.tile([P, QUAD, D], F32, name="done", bufs=3)
+            back = psum.tile([P, D], F32, name="back", tag="for_vector", bufs=6)
+            for j in range(BLOCKS):
+                nc.tensor.transpose(back[:, j * P : (j + 1) * P], spread_of[k][:, j, i * P : (i + 1) * P], ident[:])
+            row = k * QUAD + i
+            nc.vector.scalar_tensor_tensor(
+                out=done_of[k][:, i, :], in0=back[:], scalar=t_f32[:, row : row + 1], in1=kept_of[k][:, i, :],
+                op0=ALU.mult, op1=ALU.add,
+            )
+
+        bias_cols = psum.tile([P, P], BF16, name="bias_cols", tag="for_vector", bufs=6)
+        nc.tensor.transpose(bias_cols[:], bias_rows[:], ident_bf[:])
+        nc.vector.tensor_copy(out=bv_cols[:], in_=bias_cols[:, 0:BLOCKS])
+        nc.vector.tensor_copy(out=bm_cols[:], in_=bias_cols[:, BLOCKS : 2 * BLOCKS])
+
+        for k in range(-TURN_AHEAD, QUADS):
+            ahead = k + GATE_AHEAD
+            if k >= 0:
+                for j in range(BLOCKS):
+                    clamp(k, j)
+            for j in range(BLOCKS):
+                if k >= 0:
+                    noise(k, j)
+                if k + TURN_AHEAD < QUADS:
+                    turn(k + TURN_AHEAD, j)
+            if 0 <= ahead < QUADS:
+                quantise(ahead)
+            if k == -1:
+                nc.vector.tensor_copy(out=t_f32[:], in_=t_bf[:])
+                nc.vector.tensor_scalar(
+                    out=one_minus_t[:], in0=t_bf[:], scalar1=-1.0, scalar2=1.0, op0=ALU.mult, op1=ALU.add
+                )
+            if -1 <= k < QUADS - 1:
+                keep_share(k + 1)
+            for j in range(BLOCKS):
+                if k >= 0:
+                    sample(k, j)
+                if 0 <= ahead < QUADS:
+                    gate(ahead, j)
+            if 0 <= ahead < QUADS and ahead % 2 == 1:
+                log(ahead - 1)
+                log(ahead)
+            if k >= 0:
+                for i in range(QUAD):
+                    blend(k, i)
+                nc.sync.dma_start(out=out_rows[:, k * QUAD : (k + 1) * QUAD, :], in_=done_of[k][:])

@@ -21,7 +21,7 @@ QUAD = 4
 QUADS = TILES // QUAD
 BLOCKS = D // P
 LOAD = 8
-GATE_AHEAD = 3
+GATE_AHEAD = 2
 TURN_AHEAD = 4
 TINY = 2.0 ** -63
 
@@ -92,7 +92,7 @@ def tile_diffscm_pb_t_kernel(
         kept_of = {}
         done_of = {}
 
-        def turn(k, i):
+        def turn(k, i, copy):
             if i == 0:
                 grouped_of[k] = flow.tile([P, QUAD * P * 4], BF16, name="grouped", align_bytes=64)
             if i % 2 == 0:
@@ -102,7 +102,7 @@ def tile_diffscm_pb_t_kernel(
                 nc.tensor.transpose(turned_of[k][:, i % 2, h, :], words[:, h : D // 2 : 2], ident[:])
             if i % 2 == 1:
                 grouped_words = grouped_of[k][:].bitcast(F32).rearrange("p (i r h) -> p i r h", i=QUAD, r=P, h=2)
-                nc.scalar.copy(
+                copy(
                     out=grouped_words[:, i - 1 : i + 1, :, :],
                     in_=turned_of[k][:].rearrange("p i h r -> p i r h"),
                 )
@@ -127,7 +127,7 @@ def tile_diffscm_pb_t_kernel(
 
         def gate(k, j):
             if j == 0:
-                spread_of[k] = flow.tile([P, BLOCKS, QUAD * P], F32, name="spread", bufs=4)
+                spread_of[k] = flow.tile([P, BLOCKS, QUAD * P], F32, name="spread", bufs=5)
             acc = psum.tile([P, QUAD * P], F32, name="acc_gate", tag="for_scalar", bufs=2)
             head(acc, wv_words, wv_plane, j, k)
             nc.scalar.activation(
@@ -135,8 +135,9 @@ def tile_diffscm_pb_t_kernel(
             )
 
         def log(k):
-            flat = spread_of[k][:].rearrange("p j r -> p (j r)")
-            nc.scalar.activation(out=flat, in_=flat, func=ACT.Ln, bias=TINY)
+            for j in range(BLOCKS):
+                part = spread_of[k][:, j, :]
+                nc.scalar.activation(out=part, in_=part, func=ACT.Ln, bias=TINY)
 
         def clamp(k, j):
             acc = psum.tile([P, QUAD * P], F32, name="acc_clamp", tag="for_vector", bufs=6)
@@ -164,7 +165,7 @@ def tile_diffscm_pb_t_kernel(
             )
 
         def keep_share(k):
-            kept_of[k] = flow.tile([P, QUAD, D], F32, name="kept")
+            kept_of[k] = flow.tile([P, QUAD, D], F32, name="kept", bufs=3)
             for i in range(QUAD):
                 row = k * QUAD + i
                 nc.gpsimd.tensor_scalar(
@@ -174,7 +175,7 @@ def tile_diffscm_pb_t_kernel(
 
         def blend(k, i):
             if i == 0:
-                done_of[k] = flow.tile([P, QUAD, D], F32, name="done", bufs=3)
+                done_of[k] = flow.tile([P, QUAD, D], F32, name="done", bufs=2)
             back = psum.tile([P, D], F32, name="back", tag="for_vector", bufs=6)
             for j in range(BLOCKS):
                 nc.tensor.transpose(back[:, j * P : (j + 1) * P], spread_of[k][:, j, i * P : (i + 1) * P], ident[:])
@@ -189,34 +190,65 @@ def tile_diffscm_pb_t_kernel(
         nc.vector.tensor_copy(out=bv_cols[:], in_=bias_cols[:, 0:BLOCKS])
         nc.vector.tensor_copy(out=bm_cols[:], in_=bias_cols[:, BLOCKS : 2 * BLOCKS])
 
-        for k in range(-TURN_AHEAD, QUADS):
-            ahead = k + GATE_AHEAD
-            if k >= 0:
-                for j in range(BLOCKS):
-                    clamp(k, j)
-            for j in range(BLOCKS):
-                if k >= 0:
-                    noise(k, j)
-                if k + TURN_AHEAD < QUADS:
-                    turn(k + TURN_AHEAD, j)
-            if 0 <= ahead < QUADS:
-                quantise(ahead)
-            if k == -1:
+        warm = keep.tile([P, 2], F32, name="warm")
+        nc.vector.memset(warm[:], 0.0)
+
+        def valid(k):
+            return 0 <= k < QUADS
+
+        def finish(k):
+            for i in range(QUAD):
+                blend(k, i)
+                nc.sync.dma_start(out=out_rows[:, k * QUAD + i, :], in_=done_of[k][:, i, :])
+
+        for a in range(-TURN_AHEAD, QUADS + 1, 2):
+            b = a + 1
+            gated = a + GATE_AHEAD
+            turned = a + TURN_AHEAD
+            copy = nc.scalar.copy if a >= 0 else nc.vector.tensor_copy
+            if a == -2:
                 nc.vector.tensor_copy(out=t_f32[:], in_=t_bf[:])
                 nc.vector.tensor_scalar(
                     out=one_minus_t[:], in0=t_bf[:], scalar1=-1.0, scalar2=1.0, op0=ALU.mult, op1=ALU.add
                 )
-            if -1 <= k < QUADS - 1:
-                keep_share(k + 1)
+            for k in (a, b):
+                if valid(k):
+                    keep_share(k)
             for j in range(BLOCKS):
-                if k >= 0:
-                    sample(k, j)
-                if 0 <= ahead < QUADS:
-                    gate(ahead, j)
-            if 0 <= ahead < QUADS and ahead % 2 == 1:
-                log(ahead - 1)
-                log(ahead)
-            if k >= 0:
-                for i in range(QUAD):
-                    blend(k, i)
-                nc.sync.dma_start(out=out_rows[:, k * QUAD : (k + 1) * QUAD, :], in_=done_of[k][:])
+                if valid(a):
+                    clamp(a, j)
+                if valid(gated):
+                    gate(gated, j)
+            if valid(turned - 1):
+                quantise(turned - 1)
+            if valid(a - 1):
+                finish(a - 1)
+            for j in range(BLOCKS):
+                if valid(a):
+                    noise(a, j)
+                if valid(turned):
+                    turn(turned, j, copy)
+            for j in range(BLOCKS):
+                if valid(a):
+                    sample(a, j)
+                if valid(gated + 1):
+                    gate(gated + 1, j)
+            if valid(gated):
+                log(gated)
+                log(gated + 1)
+                nc.scalar.activation(out=warm[:, 1:2], in_=warm[:, 0:1], func=ACT.Sigmoid)
+            if valid(turned):
+                quantise(turned)
+            for j in range(BLOCKS):
+                if valid(b):
+                    clamp(b, j)
+            if valid(a):
+                finish(a)
+            for j in range(BLOCKS):
+                if valid(b):
+                    noise(b, j)
+                if valid(turned + 1):
+                    turn(turned + 1, j, copy)
+            for j in range(BLOCKS):
+                if valid(b):
+                    sample(b, j)

@@ -21,8 +21,9 @@ QUAD = 4
 QUADS = TILES // QUAD
 BLOCKS = D // P
 LOAD = 8
-GATE_AHEAD = 2
-TURN_AHEAD = 4
+TURN_AHEAD = 5
+S_BANKS = 3
+V_BANKS = 5
 TINY = 2.0 ** -63
 
 FLOPS = 2 * 2 * ROWS * D * D
@@ -59,23 +60,27 @@ def tile_diffscm_pb_t_kernel(
         xt_sb = keep.tile([P, TILES, D], BF16, name="xt_sb")
         eps_sb = keep.tile([P, TILES, D], BF16, name="eps_sb")
         x_sb = keep.tile([P, TILES, D], BF16, name="x_sb")
-        nc.sync.dma_start(out=xt_sb[:, 0:QUAD, :], in_=xt_rows[:, 0:QUAD, :])
+
+        def load(dst, src, k):
+            rows = slice(k * QUAD, (k + 1) * QUAD)
+            nc.sync.dma_start(out=dst[:, rows, :], in_=src[:, rows, :])
+
+        load(xt_sb, xt_rows, 0)
         wv_words, wv_plane = load_fp4_weight(nc, keep, Wv_words, Wv_scales, "wv")
         bias_rows = keep.tile([P, P], BF16, name="bias_rows")
         nc.vector.memset(bias_rows[:], 0.0)
         nc.sync.dma_start(out=bias_rows[0:BLOCKS, :], in_=bv.rearrange("(j p) -> j p", p=P))
         nc.sync.dma_start(out=bias_rows[BLOCKS : 2 * BLOCKS, :], in_=bm.rearrange("(j p) -> j p", p=P))
-        nc.sync.dma_start(out=xt_sb[:, QUAD:LOAD, :], in_=xt_rows[:, QUAD:LOAD, :])
+        load(xt_sb, xt_rows, 1)
+        load(xt_sb, xt_rows, 2)
         wm_words, wm_plane = load_fp4_weight(nc, keep, Wm_words, Wm_scales, "wm")
         t_bf = keep.tile([P, TILES], BF16, name="t_bf")
         nc.sync.dma_start(out=t_bf[:], in_=t_rand.rearrange("(p i) o -> p (i o)", i=TILES))
-        for b in range(TILES // LOAD):
-            rows = slice(b * LOAD, (b + 1) * LOAD)
-            if b + 1 < TILES // LOAD:
-                later = slice((b + 1) * LOAD, (b + 2) * LOAD)
-                nc.sync.dma_start(out=xt_sb[:, later, :], in_=xt_rows[:, later, :])
-            nc.sync.dma_start(out=eps_sb[:, rows, :], in_=eps_rows[:, rows, :])
-            nc.sync.dma_start(out=x_sb[:, rows, :], in_=x_rows[:, rows, :])
+        for k in range(QUADS):
+            if k + 3 < QUADS:
+                load(xt_sb, xt_rows, k + 3)
+            load(eps_sb, eps_rows, k)
+            load(x_sb, x_rows, k)
 
         ident = keep.tile([P, P], F32, name="ident")
         make_identity(nc, ident[:])
@@ -89,27 +94,27 @@ def tile_diffscm_pb_t_kernel(
         turned_of = {}
         codes_of = {}
         spread_of = {}
+        mean_of = {}
         kept_of = {}
-        done_of = {}
 
-        def turn(k, i, copy):
+        def turn(k, i):
             if i == 0:
                 grouped_of[k] = flow.tile([P, QUAD * P * 4], BF16, name="grouped", align_bytes=64)
             if i % 2 == 0:
-                turned_of[k] = psum.tile([P, 2, 2, P], F32, name="turned", tag="for_scalar", bufs=2)
+                turned_of[k] = psum.tile([P, 2, 2, P], F32, name="turned", tag="for_vector", bufs=V_BANKS)
             words = xt_sb[:, k * QUAD + i, :].bitcast(F32)
             for h in range(2):
                 nc.tensor.transpose(turned_of[k][:, i % 2, h, :], words[:, h : D // 2 : 2], ident[:])
             if i % 2 == 1:
                 grouped_words = grouped_of[k][:].bitcast(F32).rearrange("p (i r h) -> p i r h", i=QUAD, r=P, h=2)
-                copy(
+                nc.vector.tensor_copy(
                     out=grouped_words[:, i - 1 : i + 1, :, :],
                     in_=turned_of[k][:].rearrange("p i h r -> p i r h"),
                 )
 
         def quantise(k):
-            codes = flow.tile([P, QUAD * P], U32, name="codes", bufs=5, align_bytes=64)
-            planes = flow.tile([P, QUAD * P], U8, name="planes", bufs=5, align_bytes=64)
+            codes = flow.tile([P, QUAD * P], U32, name="codes", bufs=QUADS, align_bytes=64)
+            planes = flow.tile([P, QUAD * P], U8, name="planes", bufs=QUADS, align_bytes=64)
             nc.vector.quantize_mx(out=codes[:].bitcast(FP8X4), scales=planes[:], in_=grouped_of[k][:])
             codes_of[k] = (codes, planes)
 
@@ -128,7 +133,7 @@ def tile_diffscm_pb_t_kernel(
         def gate(k, j):
             if j == 0:
                 spread_of[k] = flow.tile([P, BLOCKS, QUAD * P], F32, name="spread", bufs=5)
-            acc = psum.tile([P, QUAD * P], F32, name="acc_gate", tag="for_scalar", bufs=2)
+            acc = psum.tile([P, QUAD * P], F32, name="acc_gate", tag="for_scalar", bufs=S_BANKS)
             head(acc, wv_words, wv_plane, j, k)
             nc.scalar.activation(
                 out=spread_of[k][:, j, :], in_=acc[:], func=ACT.Sigmoid, bias=bv_cols[:, j : j + 1]
@@ -139,8 +144,17 @@ def tile_diffscm_pb_t_kernel(
                 part = spread_of[k][:, j, :]
                 nc.scalar.activation(out=part, in_=part, func=ACT.Ln, bias=TINY)
 
+        def mean(k, j):
+            if j == 0:
+                mean_of[k] = flow.tile([P, BLOCKS, QUAD * P], F32, name="mean", bufs=3)
+            acc = psum.tile([P, QUAD * P], F32, name="acc_mean", tag="for_scalar", bufs=S_BANKS)
+            head(acc, wm_words, wm_plane, j, k)
+            nc.scalar.activation(
+                out=mean_of[k][:, j, :], in_=acc[:], func=ACT.Identity, bias=bm_cols[:, j : j + 1]
+            )
+
         def clamp(k, j):
-            acc = psum.tile([P, QUAD * P], F32, name="acc_clamp", tag="for_vector", bufs=6)
+            acc = psum.tile([P, QUAD * P], F32, name="acc_clamp", tag="for_vector", bufs=V_BANKS)
             head(acc, wv_words, wv_plane, j, k)
             part = spread_of[k][:, j, :]
             nc.vector.scalar_tensor_tensor(
@@ -148,7 +162,7 @@ def tile_diffscm_pb_t_kernel(
             )
 
         def noise(k, j):
-            eps_t = psum.tile([P, QUAD * P], BF16, name="eps_t", tag="for_vector", bufs=6)
+            eps_t = psum.tile([P, QUAD * P], BF16, name="eps_t", tag="for_vector", bufs=V_BANKS)
             for i in range(QUAD):
                 nc.tensor.transpose(
                     eps_t[:, i * P : (i + 1) * P], eps_sb[:, k * QUAD + i, j * P : (j + 1) * P], ident_bf[:]
@@ -156,16 +170,8 @@ def tile_diffscm_pb_t_kernel(
             part = spread_of[k][:, j, :]
             nc.vector.scalar_tensor_tensor(out=part, in0=part, scalar=0.0, in1=eps_t[:], op0=ALU.max, op1=ALU.mult)
 
-        def sample(k, j):
-            acc = psum.tile([P, QUAD * P], F32, name="acc_mean", tag="for_vector", bufs=6)
-            head(acc, wm_words, wm_plane, j, k)
-            part = spread_of[k][:, j, :]
-            nc.vector.scalar_tensor_tensor(
-                out=part, in0=acc[:], scalar=bm_cols[:, j : j + 1], in1=part, op0=ALU.add, op1=ALU.add
-            )
-
         def keep_share(k):
-            kept_of[k] = flow.tile([P, QUAD, D], F32, name="kept", bufs=3)
+            kept_of[k] = flow.tile([P, QUAD, D], F32, name="kept", bufs=4)
             for i in range(QUAD):
                 row = k * QUAD + i
                 nc.gpsimd.tensor_scalar(
@@ -174,24 +180,32 @@ def tile_diffscm_pb_t_kernel(
                 )
 
         def blend(k, i):
-            if i == 0:
-                done_of[k] = flow.tile([P, QUAD, D], F32, name="done", bufs=2)
-            back = psum.tile([P, D], F32, name="back", tag="for_vector", bufs=6)
+            back = psum.tile([P, D], F32, name="back", tag="for_vector", bufs=V_BANKS)
+            rows = slice(i * P, (i + 1) * P)
             for j in range(BLOCKS):
-                nc.tensor.transpose(back[:, j * P : (j + 1) * P], spread_of[k][:, j, i * P : (i + 1) * P], ident[:])
+                cols = slice(j * P, (j + 1) * P)
+                nc.tensor.matmul(
+                    out=back[:, cols], lhsT=mean_of[k][:, j, rows], rhs=ident[:], is_transpose=True,
+                    start=True, stop=False,
+                )
+                nc.tensor.matmul(
+                    out=back[:, cols], lhsT=spread_of[k][:, j, rows], rhs=ident[:], is_transpose=True,
+                    start=False, stop=True,
+                )
             row = k * QUAD + i
             nc.vector.scalar_tensor_tensor(
-                out=done_of[k][:, i, :], in0=back[:], scalar=t_f32[:, row : row + 1], in1=kept_of[k][:, i, :],
+                out=kept_of[k][:, i, :], in0=back[:], scalar=t_f32[:, row : row + 1], in1=kept_of[k][:, i, :],
                 op0=ALU.mult, op1=ALU.add,
             )
 
-        bias_cols = psum.tile([P, P], BF16, name="bias_cols", tag="for_vector", bufs=6)
+        warm = keep.tile([P, 2], F32, name="warm")
+        nc.vector.memset(warm[:], 0.0)
+        nc.scalar.activation(out=warm[:, 1:2], in_=warm[:, 0:1], func=ACT.Sigmoid)
+
+        bias_cols = psum.tile([P, P], BF16, name="bias_cols", tag="for_vector", bufs=V_BANKS)
         nc.tensor.transpose(bias_cols[:], bias_rows[:], ident_bf[:])
         nc.vector.tensor_copy(out=bv_cols[:], in_=bias_cols[:, 0:BLOCKS])
         nc.vector.tensor_copy(out=bm_cols[:], in_=bias_cols[:, BLOCKS : 2 * BLOCKS])
-
-        warm = keep.tile([P, 2], F32, name="warm")
-        nc.vector.memset(warm[:], 0.0)
 
         def valid(k):
             return 0 <= k < QUADS
@@ -199,56 +213,53 @@ def tile_diffscm_pb_t_kernel(
         def finish(k):
             for i in range(QUAD):
                 blend(k, i)
-                nc.sync.dma_start(out=out_rows[:, k * QUAD + i, :], in_=done_of[k][:, i, :])
+                nc.sync.dma_start(out=out_rows[:, k * QUAD + i, :], in_=kept_of[k][:, i, :])
 
-        for a in range(-TURN_AHEAD, QUADS + 1, 2):
+        for a in range(-TURN_AHEAD - 1, QUADS + 1, 2):
             b = a + 1
-            gated = a + GATE_AHEAD
-            turned = a + TURN_AHEAD
-            copy = nc.scalar.copy if a >= 0 else nc.vector.tensor_copy
             if a == -2:
                 nc.vector.tensor_copy(out=t_f32[:], in_=t_bf[:])
                 nc.vector.tensor_scalar(
                     out=one_minus_t[:], in0=t_bf[:], scalar1=-1.0, scalar2=1.0, op0=ALU.mult, op1=ALU.add
                 )
-            for k in (a, b):
+            for k in (a + 1, a + 2):
                 if valid(k):
                     keep_share(k)
             for j in range(BLOCKS):
                 if valid(a):
                     clamp(a, j)
-                if valid(gated):
-                    gate(gated, j)
-            if valid(turned - 1):
-                quantise(turned - 1)
+                if valid(a + 2):
+                    gate(a + 2, j)
+                if valid(a + 3):
+                    gate(a + 3, j)
+            if valid(a + TURN_AHEAD - 1):
+                quantise(a + TURN_AHEAD - 1)
+            if valid(a + 2):
+                log(a + 2)
             if valid(a - 1):
                 finish(a - 1)
             for j in range(BLOCKS):
                 if valid(a):
                     noise(a, j)
-                if valid(turned):
-                    turn(turned, j, copy)
-            for j in range(BLOCKS):
-                if valid(a):
-                    sample(a, j)
-                if valid(gated + 1):
-                    gate(gated + 1, j)
-            if valid(gated):
-                log(gated)
-                log(gated + 1)
-                nc.scalar.activation(out=warm[:, 1:2], in_=warm[:, 0:1], func=ACT.Sigmoid)
-            if valid(turned):
-                quantise(turned)
+                if valid(a + TURN_AHEAD):
+                    turn(a + TURN_AHEAD, j)
             for j in range(BLOCKS):
                 if valid(b):
                     clamp(b, j)
+                if valid(a + 1):
+                    mean(a + 1, j)
+                if valid(a + 2):
+                    mean(a + 2, j)
+            if valid(a + TURN_AHEAD):
+                quantise(a + TURN_AHEAD)
+            if valid(a + 3):
+                log(a + 3)
+                if valid(a + 4):
+                    nc.scalar.activation(out=warm[:, 1:2], in_=warm[:, 0:1], func=ACT.Sigmoid)
             if valid(a):
                 finish(a)
             for j in range(BLOCKS):
                 if valid(b):
                     noise(b, j)
-                if valid(turned + 1):
-                    turn(turned + 1, j, copy)
-            for j in range(BLOCKS):
-                if valid(b):
-                    sample(b, j)
+                if valid(a + TURN_AHEAD + 1):
+                    turn(a + TURN_AHEAD + 1, j)

@@ -22,8 +22,9 @@ QUADS = TILES // QUAD
 BLOCKS = D // P
 LOAD = 8
 TURN_AHEAD = 5
-S_BANKS = 3
-V_BANKS = 5
+S_BANKS = 4
+V_BANKS = 4
+ON_VECTOR = (3,)
 TINY = 2.0 ** -63
 
 FLOPS = 2 * 2 * ROWS * D * D
@@ -76,11 +77,15 @@ def tile_diffscm_pb_t_kernel(
         wm_words, wm_plane = load_fp4_weight(nc, keep, Wm_words, Wm_scales, "wm")
         t_bf = keep.tile([P, TILES], BF16, name="t_bf")
         nc.sync.dma_start(out=t_bf[:], in_=t_rand.rearrange("(p i) o -> p (i o)", i=TILES))
+        load(xt_sb, xt_rows, 3)
+        load(xt_sb, xt_rows, 4)
         for k in range(QUADS):
-            if k + 3 < QUADS:
-                load(xt_sb, xt_rows, k + 3)
             load(eps_sb, eps_rows, k)
             load(x_sb, x_rows, k)
+            if k % 2 == 1 and k // 2 + 5 < QUADS:
+                load(xt_sb, xt_rows, k // 2 + 5)
+                if k == 1:
+                    load(xt_sb, xt_rows, 7)
 
         ident = keep.tile([P, P], F32, name="ident")
         make_identity(nc, ident[:])
@@ -97,17 +102,21 @@ def tile_diffscm_pb_t_kernel(
         mean_of = {}
         kept_of = {}
 
-        def turn(k, i):
+        def turn(k, i, by_scalar):
             if i == 0:
-                grouped_of[k] = flow.tile([P, QUAD * P * 4], BF16, name="grouped", align_bytes=64)
+                grouped_of[k] = flow.tile([P, QUAD * P * 4], BF16, name="grouped", bufs=3, align_bytes=64)
             if i % 2 == 0:
-                turned_of[k] = psum.tile([P, 2, 2, P], F32, name="turned", tag="for_vector", bufs=V_BANKS)
+                if by_scalar:
+                    turned_of[k] = psum.tile([P, 2, 2, P], F32, name="turned_s", tag="for_scalar", bufs=S_BANKS)
+                else:
+                    turned_of[k] = psum.tile([P, 2, 2, P], F32, name="turned", tag="for_vector", bufs=V_BANKS)
             words = xt_sb[:, k * QUAD + i, :].bitcast(F32)
             for h in range(2):
                 nc.tensor.transpose(turned_of[k][:, i % 2, h, :], words[:, h : D // 2 : 2], ident[:])
             if i % 2 == 1:
                 grouped_words = grouped_of[k][:].bitcast(F32).rearrange("p (i r h) -> p i r h", i=QUAD, r=P, h=2)
-                nc.vector.tensor_copy(
+                copy = nc.scalar.copy if by_scalar else nc.vector.tensor_copy
+                copy(
                     out=grouped_words[:, i - 1 : i + 1, :, :],
                     in_=turned_of[k][:].rearrange("p i h r -> p i r h"),
                 )
@@ -132,7 +141,7 @@ def tile_diffscm_pb_t_kernel(
 
         def gate(k, j):
             if j == 0:
-                spread_of[k] = flow.tile([P, BLOCKS, QUAD * P], F32, name="spread", bufs=5)
+                spread_of[k] = flow.tile([P, BLOCKS, QUAD * P], F32, name="spread", bufs=4)
             acc = psum.tile([P, QUAD * P], F32, name="acc_gate", tag="for_scalar", bufs=S_BANKS)
             head(acc, wv_words, wv_plane, j, k)
             nc.scalar.activation(
@@ -170,6 +179,14 @@ def tile_diffscm_pb_t_kernel(
             part = spread_of[k][:, j, :]
             nc.vector.scalar_tensor_tensor(out=part, in0=part, scalar=0.0, in1=eps_t[:], op0=ALU.max, op1=ALU.mult)
 
+        def sample(k, j):
+            acc = psum.tile([P, QUAD * P], F32, name="acc_sample", tag="for_vector", bufs=V_BANKS)
+            head(acc, wm_words, wm_plane, j, k)
+            part = spread_of[k][:, j, :]
+            nc.vector.scalar_tensor_tensor(
+                out=part, in0=acc[:], scalar=bm_cols[:, j : j + 1], in1=part, op0=ALU.add, op1=ALU.add
+            )
+
         def keep_share(k):
             kept_of[k] = flow.tile([P, QUAD, D], F32, name="kept", bufs=4)
             for i in range(QUAD):
@@ -184,13 +201,14 @@ def tile_diffscm_pb_t_kernel(
             rows = slice(i * P, (i + 1) * P)
             for j in range(BLOCKS):
                 cols = slice(j * P, (j + 1) * P)
-                nc.tensor.matmul(
-                    out=back[:, cols], lhsT=mean_of[k][:, j, rows], rhs=ident[:], is_transpose=True,
-                    start=True, stop=False,
-                )
+                if j not in ON_VECTOR:
+                    nc.tensor.matmul(
+                        out=back[:, cols], lhsT=mean_of[k][:, j, rows], rhs=ident[:], is_transpose=True,
+                        start=True, stop=False,
+                    )
                 nc.tensor.matmul(
                     out=back[:, cols], lhsT=spread_of[k][:, j, rows], rhs=ident[:], is_transpose=True,
-                    start=False, stop=True,
+                    start=j in ON_VECTOR, stop=True,
                 )
             row = k * QUAD + i
             nc.vector.scalar_tensor_tensor(
@@ -215,51 +233,61 @@ def tile_diffscm_pb_t_kernel(
                 blend(k, i)
                 nc.sync.dma_start(out=out_rows[:, k * QUAD + i, :], in_=kept_of[k][:, i, :])
 
-        for a in range(-TURN_AHEAD - 1, QUADS + 1, 2):
+        on_scalar = [j for j in range(BLOCKS) if j not in ON_VECTOR]
+
+        def turn_quad(k):
+            for i in range(QUAD):
+                turn(k, i, False)
+                if i == 1 and valid(k - 1):
+                    quantise(k - 1)
+
+        for a in range(-TURN_AHEAD - 1, QUADS, 2):
             b = a + 1
             if a == -2:
                 nc.vector.tensor_copy(out=t_f32[:], in_=t_bf[:])
                 nc.vector.tensor_scalar(
                     out=one_minus_t[:], in0=t_bf[:], scalar1=-1.0, scalar2=1.0, op0=ALU.mult, op1=ALU.add
                 )
-            for k in (a + 1, a + 2):
+            for k in (a + 2, a + 3):
                 if valid(k):
                     keep_share(k)
-            for j in range(BLOCKS):
-                if valid(a):
-                    clamp(a, j)
-                if valid(a + 2):
-                    gate(a + 2, j)
-                if valid(a + 3):
-                    gate(a + 3, j)
-            if valid(a + TURN_AHEAD - 1):
-                quantise(a + TURN_AHEAD - 1)
-            if valid(a + 2):
-                log(a + 2)
-            if valid(a - 1):
-                finish(a - 1)
-            for j in range(BLOCKS):
-                if valid(a):
+            late = [k for k in (a + TURN_AHEAD, a + TURN_AHEAD + 1) if valid(k)]
+            if valid(a):
+                for k in (a, b):
+                    for j in range(BLOCKS):
+                        clamp(k, j)
+                if a == 0:
+                    quantise(TURN_AHEAD - 1)
+                for j in on_scalar:
+                    mean(a, j)
+                for j in range(BLOCKS):
                     noise(a, j)
-                if valid(a + TURN_AHEAD):
-                    turn(a + TURN_AHEAD, j)
-            for j in range(BLOCKS):
-                if valid(b):
-                    clamp(b, j)
-                if valid(a + 1):
-                    mean(a + 1, j)
+                for j in on_scalar:
+                    mean(b, j)
+                for j in range(BLOCKS):
+                    noise(b, j)
+                for k in late:
+                    for i in range(QUAD):
+                        turn(k, i, True)
                 if valid(a + 2):
-                    mean(a + 2, j)
-            if valid(a + TURN_AHEAD):
-                quantise(a + TURN_AHEAD)
-            if valid(a + 3):
-                log(a + 3)
-                if valid(a + 4):
                     nc.scalar.activation(out=warm[:, 1:2], in_=warm[:, 0:1], func=ACT.Sigmoid)
+                for k in (a, b):
+                    for j in ON_VECTOR:
+                        sample(k, j)
+            if valid(a + 2):
+                for j in range(BLOCKS):
+                    gate(a + 2, j)
             if valid(a):
                 finish(a)
-            for j in range(BLOCKS):
-                if valid(b):
-                    noise(b, j)
-                if valid(a + TURN_AHEAD + 1):
-                    turn(a + TURN_AHEAD + 1, j)
+                for k in late:
+                    quantise(k)
+            if valid(a + 2):
+                for j in range(BLOCKS):
+                    gate(a + 3, j)
+                log(a + 2)
+                log(a + 3)
+            if valid(a):
+                finish(b)
+            else:
+                for k in late:
+                    turn_quad(k)

@@ -25,6 +25,7 @@ TURN_AHEAD = 5
 S_BANKS = 4
 V_BANKS = 4
 ON_VECTOR = (3,)
+ON_POOL = (0, 1, 2)
 TINY = 2.0 ** -63
 
 FLOPS = 2 * 2 * ROWS * D * D
@@ -187,6 +188,10 @@ def tile_diffscm_pb_t_kernel(
                 out=part, in0=acc[:], scalar=bm_cols[:, j : j + 1], in1=part, op0=ALU.add, op1=ALU.add
             )
 
+        def pool_add(k, j):
+            part = spread_of[k][:, j, :]
+            nc.gpsimd.tensor_tensor(out=part, in0=part, in1=mean_of[k][:, j, :], op=ALU.add)
+
         def keep_share(k):
             kept_of[k] = flow.tile([P, QUAD, D], F32, name="kept", bufs=4)
             for i in range(QUAD):
@@ -201,14 +206,14 @@ def tile_diffscm_pb_t_kernel(
             rows = slice(i * P, (i + 1) * P)
             for j in range(BLOCKS):
                 cols = slice(j * P, (j + 1) * P)
-                if j not in ON_VECTOR:
+                if j not in ON_VECTOR and j not in ON_POOL:
                     nc.tensor.matmul(
                         out=back[:, cols], lhsT=mean_of[k][:, j, rows], rhs=ident[:], is_transpose=True,
                         start=True, stop=False,
                     )
                 nc.tensor.matmul(
                     out=back[:, cols], lhsT=spread_of[k][:, j, rows], rhs=ident[:], is_transpose=True,
-                    start=j in ON_VECTOR, stop=True,
+                    start=j in ON_VECTOR or j in ON_POOL, stop=True,
                 )
             row = k * QUAD + i
             nc.vector.scalar_tensor_tensor(
@@ -248,9 +253,10 @@ def tile_diffscm_pb_t_kernel(
                 nc.vector.tensor_scalar(
                     out=one_minus_t[:], in0=t_bf[:], scalar1=-1.0, scalar2=1.0, op0=ALU.mult, op1=ALU.add
                 )
-            for k in (a + 2, a + 3):
-                if valid(k):
-                    keep_share(k)
+            if not valid(a):
+                for k in (a + 2, a + 3):
+                    if valid(k):
+                        keep_share(k)
             late = [k for k in (a + TURN_AHEAD, a + TURN_AHEAD + 1) if valid(k)]
             if valid(a):
                 for k in (a, b):
@@ -262,10 +268,17 @@ def tile_diffscm_pb_t_kernel(
                     mean(a, j)
                 for j in range(BLOCKS):
                     noise(a, j)
+                    if j in ON_POOL:
+                        pool_add(a, j)
                 for j in on_scalar:
                     mean(b, j)
                 for j in range(BLOCKS):
                     noise(b, j)
+                    if j in ON_POOL:
+                        pool_add(b, j)
+                for k in (a + 2, a + 3):
+                    if valid(k):
+                        keep_share(k)
                 for k in late:
                     for i in range(QUAD):
                         turn(k, i, True)

@@ -21,11 +21,13 @@ QUAD = 4
 QUADS = TILES // QUAD
 BLOCKS = D // P
 LOAD = 8
-TURN_AHEAD = 5
+HEAD_QUADS = 5
 S_BANKS = 4
 V_BANKS = 4
 ON_VECTOR = (3,)
-ON_POOL = (0, 1, 2)
+LOG_PARTS = 2
+ON_POOL = (0, 1, 2, 3)
+LAST_POOL = ()
 TINY = 2.0 ** -63
 
 FLOPS = 2 * 2 * ROWS * D * D
@@ -83,10 +85,9 @@ def tile_diffscm_pb_t_kernel(
         for k in range(QUADS):
             load(eps_sb, eps_rows, k)
             load(x_sb, x_rows, k)
-            if k % 2 == 1 and k // 2 + 5 < QUADS:
-                load(xt_sb, xt_rows, k // 2 + 5)
-                if k == 1:
-                    load(xt_sb, xt_rows, 7)
+            if k == 1:
+                for later in range(HEAD_QUADS, QUADS):
+                    load(xt_sb, xt_rows, later)
 
         ident = keep.tile([P, P], F32, name="ident")
         make_identity(nc, ident[:])
@@ -150,8 +151,9 @@ def tile_diffscm_pb_t_kernel(
             )
 
         def log(k):
-            for j in range(BLOCKS):
-                part = spread_of[k][:, j, :]
+            for half in range(LOG_PARTS):
+                blocks = slice(half * BLOCKS // LOG_PARTS, (half + 1) * BLOCKS // LOG_PARTS)
+                part = spread_of[k][:, blocks, :]
                 nc.scalar.activation(out=part, in_=part, func=ACT.Ln, bias=TINY)
 
         def mean(k, j):
@@ -201,19 +203,25 @@ def tile_diffscm_pb_t_kernel(
                     op0=ALU.mult, op1=ALU.add,
                 )
 
+        def by_vector(k):
+            return ON_VECTOR if k < QUADS - 2 else ()
+
+        def by_pool(k):
+            return ON_POOL if k < QUADS - 2 else LAST_POOL
+
         def blend(k, i):
             back = psum.tile([P, D], F32, name="back", tag="for_vector", bufs=V_BANKS)
             rows = slice(i * P, (i + 1) * P)
             for j in range(BLOCKS):
                 cols = slice(j * P, (j + 1) * P)
-                if j not in ON_VECTOR and j not in ON_POOL:
+                if j not in by_vector(k) and j not in by_pool(k):
                     nc.tensor.matmul(
                         out=back[:, cols], lhsT=mean_of[k][:, j, rows], rhs=ident[:], is_transpose=True,
                         start=True, stop=False,
                     )
                 nc.tensor.matmul(
                     out=back[:, cols], lhsT=spread_of[k][:, j, rows], rhs=ident[:], is_transpose=True,
-                    start=j in ON_VECTOR or j in ON_POOL, stop=True,
+                    start=j in by_vector(k) or j in by_pool(k), stop=True,
                 )
             row = k * QUAD + i
             nc.vector.scalar_tensor_tensor(
@@ -238,69 +246,67 @@ def tile_diffscm_pb_t_kernel(
                 blend(k, i)
                 nc.sync.dma_start(out=out_rows[:, k * QUAD + i, :], in_=kept_of[k][:, i, :])
 
-        on_scalar = [j for j in range(BLOCKS) if j not in ON_VECTOR]
 
         def turn_quad(k):
             for i in range(QUAD):
                 turn(k, i, False)
-                if i == 1 and valid(k - 1):
+                if i == 1 and valid(k - 1) and k - 1 not in codes_of:
                     quantise(k - 1)
 
-        for a in range(-TURN_AHEAD - 1, QUADS, 2):
+        def gates(k):
+            for j in range(BLOCKS):
+                gate(k, j)
+
+        turn_quad(0)
+        quantise(0)
+        turn_quad(1)
+        quantise(1)
+        gates(0)
+        turn_quad(2)
+        gates(1)
+        log(0)
+        log(1)
+        nc.vector.tensor_copy(out=t_f32[:], in_=t_bf[:])
+        nc.vector.tensor_scalar(out=one_minus_t[:], in0=t_bf[:], scalar1=-1.0, scalar2=1.0, op0=ALU.mult, op1=ALU.add)
+        keep_share(0)
+        keep_share(1)
+        for k in range(3, HEAD_QUADS):
+            turn_quad(k)
+
+        for a in range(0, QUADS, 2):
             b = a + 1
-            if a == -2:
-                nc.vector.tensor_copy(out=t_f32[:], in_=t_bf[:])
-                nc.vector.tensor_scalar(
-                    out=one_minus_t[:], in0=t_bf[:], scalar1=-1.0, scalar2=1.0, op0=ALU.mult, op1=ALU.add
-                )
-            if not valid(a):
-                for k in (a + 2, a + 3):
-                    if valid(k):
-                        keep_share(k)
-            late = [k for k in (a + TURN_AHEAD, a + TURN_AHEAD + 1) if valid(k)]
-            if valid(a):
-                for k in (a, b):
-                    for j in range(BLOCKS):
-                        clamp(k, j)
-                if a == 0:
-                    quantise(TURN_AHEAD - 1)
-                for j in on_scalar:
-                    mean(a, j)
+            more = valid(a + 2)
+            for k in (a, b):
                 for j in range(BLOCKS):
-                    noise(a, j)
-                    if j in ON_POOL:
-                        pool_add(a, j)
-                for j in on_scalar:
-                    mean(b, j)
+                    clamp(k, j)
+            if a == 0:
+                quantise(HEAD_QUADS - 1)
+            for k in (a, b):
                 for j in range(BLOCKS):
-                    noise(b, j)
-                    if j in ON_POOL:
-                        pool_add(b, j)
-                for k in (a + 2, a + 3):
-                    if valid(k):
-                        keep_share(k)
-                for k in late:
-                    for i in range(QUAD):
-                        turn(k, i, True)
-                if valid(a + 2):
-                    nc.scalar.activation(out=warm[:, 1:2], in_=warm[:, 0:1], func=ACT.Sigmoid)
-                for k in (a, b):
-                    for j in ON_VECTOR:
-                        sample(k, j)
-            if valid(a + 2):
+                    if j not in by_vector(k):
+                        mean(k, j)
                 for j in range(BLOCKS):
-                    gate(a + 2, j)
-            if valid(a):
-                finish(a)
-                for k in late:
-                    quantise(k)
-            if valid(a + 2):
-                for j in range(BLOCKS):
-                    gate(a + 3, j)
+                    noise(k, j)
+                    if j not in by_vector(k) and j in by_pool(k):
+                        pool_add(k, j)
+            for k in (a + 2, a + 3):
+                if valid(k):
+                    keep_share(k)
+            if more:
+                nc.scalar.activation(out=warm[:, 1:2], in_=warm[:, 0:1], func=ACT.Sigmoid)
+            for k in (a, b):
+                for j in by_vector(k):
+                    sample(k, j)
+            if more:
+                gates(a + 2)
+            finish(a)
+            if more:
+                gates(a + 3)
                 log(a + 2)
                 log(a + 3)
-            if valid(a):
-                finish(b)
-            else:
-                for k in late:
+            finish(b)
+            for k in (HEAD_QUADS + a, HEAD_QUADS + a + 1):
+                if valid(k):
                     turn_quad(k)
+                    if k == QUADS - 1:
+                        quantise(k)

@@ -26,7 +26,7 @@ S_BANKS = 4
 V_BANKS = 4
 ON_VECTOR = (3,)
 LOG_PARTS = 2
-ON_POOL = (0, 1, 2, 3)
+ON_POOL = (0,)
 LAST_POOL = ()
 TINY = 2.0 ** -63
 

@@ -21,6 +21,7 @@ QUAD = 4
 QUADS = TILES // QUAD
 BLOCKS = D // P
 LOAD = 8
+WARM_FIRST = 6
 HEAD_QUADS = 5
 S_BANKS = 4
 V_BANKS = 4
@@ -69,7 +70,8 @@ def tile_diffscm_pb_t_kernel(
             rows = slice(k * QUAD, (k + 1) * QUAD)
             nc.sync.dma_start(out=dst[:, rows, :], in_=src[:, rows, :])
 
-        load(xt_sb, xt_rows, 0)
+        nc.sync.dma_start(out=xt_sb[:, 0:2, :], in_=xt_rows[:, 0:2, :])
+        nc.sync.dma_start(out=xt_sb[:, 2:QUAD, :], in_=xt_rows[:, 2:QUAD, :])
         wv_words, wv_plane = load_fp4_weight(nc, keep, Wv_words, Wv_scales, "wv")
         bias_rows = keep.tile([P, P], BF16, name="bias_rows")
         nc.vector.memset(bias_rows[:], 0.0)
@@ -229,14 +231,18 @@ def tile_diffscm_pb_t_kernel(
                 op0=ALU.mult, op1=ALU.add,
             )
 
+        zeros = keep.tile([P, D], BF16, name="zeros")
+        nc.vector.memset(zeros[:], 0.0)
+
+        def idle_work(n):
+            for spare_pass in range(n):
+                spare = psum.tile([P, D], F32, name="spare", tag="for_scalar", bufs=S_BANKS)
+                nc.tensor.matmul(out=spare[:], lhsT=zeros[:, 0:P], rhs=zeros[:], start=True, stop=True)
+
+        idle_work(WARM_FIRST)
         warm = keep.tile([P, 2], F32, name="warm")
         nc.vector.memset(warm[:], 0.0)
         nc.scalar.activation(out=warm[:, 1:2], in_=warm[:, 0:1], func=ACT.Sigmoid)
-
-        bias_cols = psum.tile([P, P], BF16, name="bias_cols", tag="for_vector", bufs=V_BANKS)
-        nc.tensor.transpose(bias_cols[:], bias_rows[:], ident_bf[:])
-        nc.vector.tensor_copy(out=bv_cols[:], in_=bias_cols[:, 0:BLOCKS])
-        nc.vector.tensor_copy(out=bm_cols[:], in_=bias_cols[:, BLOCKS : 2 * BLOCKS])
 
         def valid(k):
             return 0 <= k < QUADS
@@ -258,6 +264,10 @@ def tile_diffscm_pb_t_kernel(
                 gate(k, j)
 
         turn_quad(0)
+        bias_cols = psum.tile([P, P], BF16, name="bias_cols", tag="for_vector", bufs=V_BANKS)
+        nc.tensor.transpose(bias_cols[:], bias_rows[:], ident_bf[:])
+        nc.vector.tensor_copy(out=bv_cols[:], in_=bias_cols[:, 0:BLOCKS])
+        nc.vector.tensor_copy(out=bm_cols[:], in_=bias_cols[:, BLOCKS : 2 * BLOCKS])
         quantise(0)
         turn_quad(1)
         quantise(1)

@@ -25,7 +25,7 @@ WARM_FIRST = 6
 HEAD_QUADS = 5
 S_BANKS = 4
 V_BANKS = 4
-ON_VECTOR = (3,)
+ON_VECTOR = ()
 LOG_PARTS = 2
 ON_POOL = (0,)
 LAST_POOL = ()

@@ -72,18 +72,17 @@ def tile_diffscm_pb_t_kernel(
 
         nc.sync.dma_start(out=xt_sb[:, 0:2, :], in_=xt_rows[:, 0:2, :])
         nc.sync.dma_start(out=xt_sb[:, 2:QUAD, :], in_=xt_rows[:, 2:QUAD, :])
+        load(xt_sb, xt_rows, 1)
         wv_words, wv_plane = load_fp4_weight(nc, keep, Wv_words, Wv_scales, "wv")
         bias_rows = keep.tile([P, P], BF16, name="bias_rows")
         nc.vector.memset(bias_rows[:], 0.0)
-        nc.sync.dma_start(out=bias_rows[0:BLOCKS, :], in_=bv.rearrange("(j p) -> j p", p=P))
-        nc.sync.dma_start(out=bias_rows[BLOCKS : 2 * BLOCKS, :], in_=bm.rearrange("(j p) -> j p", p=P))
-        load(xt_sb, xt_rows, 1)
-        load(xt_sb, xt_rows, 2)
-        wm_words, wm_plane = load_fp4_weight(nc, keep, Wm_words, Wm_scales, "wm")
+        nc.scalar.dma_start(out=bias_rows[0:BLOCKS, :], in_=bv.rearrange("(j p) -> j p", p=P))
+        nc.scalar.dma_start(out=bias_rows[BLOCKS : 2 * BLOCKS, :], in_=bm.rearrange("(j p) -> j p", p=P))
         t_bf = keep.tile([P, TILES], BF16, name="t_bf")
-        nc.sync.dma_start(out=t_bf[:], in_=t_rand.rearrange("(p i) o -> p (i o)", i=TILES))
-        load(xt_sb, xt_rows, 3)
-        load(xt_sb, xt_rows, 4)
+        nc.scalar.dma_start(out=t_bf[:], in_=t_rand.rearrange("(p i) o -> p (i o)", i=TILES))
+        for k in range(2, HEAD_QUADS):
+            load(xt_sb, xt_rows, k)
+        wm_words, wm_plane = load_fp4_weight(nc, keep, Wm_words, Wm_scales, "wm")
         for k in range(QUADS):
             load(eps_sb, eps_rows, k)
             load(x_sb, x_rows, k)
@@ -175,13 +174,15 @@ def tile_diffscm_pb_t_kernel(
                 out=part, in0=acc[:], scalar=bv_cols[:, j : j + 1], in1=part, op0=ALU.add, op1=ALU.subtract
             )
 
-        def noise(k, j):
-            eps_t = psum.tile([P, QUAD * P], BF16, name="eps_t", tag="for_vector", bufs=V_BANKS)
-            for i in range(QUAD):
-                nc.tensor.transpose(
-                    eps_t[:, i * P : (i + 1) * P], eps_sb[:, k * QUAD + i, j * P : (j + 1) * P], ident_bf[:]
-                )
-            part = spread_of[k][:, j, :]
+        def noise(k, half):
+            eps_t = psum.tile([P, 2, QUAD * P], BF16, name="eps_t", tag="for_vector", bufs=V_BANKS)
+            for h in range(2):
+                j = 2 * half + h
+                for i in range(QUAD):
+                    nc.tensor.transpose(
+                        eps_t[:, h, i * P : (i + 1) * P], eps_sb[:, k * QUAD + i, j * P : (j + 1) * P], ident_bf[:]
+                    )
+            part = spread_of[k][:, 2 * half : 2 * half + 2, :]
             nc.vector.scalar_tensor_tensor(out=part, in0=part, scalar=0.0, in1=eps_t[:], op0=ALU.max, op1=ALU.mult)
 
         def sample(k, j):
@@ -286,6 +287,9 @@ def tile_diffscm_pb_t_kernel(
         for a in range(0, QUADS, 2):
             b = a + 1
             more = valid(a + 2)
+            for j in range(BLOCKS):
+                if j not in by_vector(a):
+                    mean(a, j)
             for k in (a, b):
                 for j in range(BLOCKS):
                     clamp(k, j)
@@ -293,12 +297,13 @@ def tile_diffscm_pb_t_kernel(
                 quantise(HEAD_QUADS - 1)
             for k in (a, b):
                 for j in range(BLOCKS):
-                    if j not in by_vector(k):
+                    if k == b and j not in by_vector(k):
                         mean(k, j)
-                for j in range(BLOCKS):
-                    noise(k, j)
-                    if j not in by_vector(k) and j in by_pool(k):
-                        pool_add(k, j)
+                for half in range(2):
+                    noise(k, half)
+                    for j in (2 * half, 2 * half + 1):
+                        if j not in by_vector(k) and j in by_pool(k):
+                            pool_add(k, j)
             for k in (a + 2, a + 3):
                 if valid(k):
                     keep_share(k)

@@ -25,7 +25,7 @@ WARM_FIRST = 6
 HEAD_QUADS = 5
 S_BANKS = 4
 V_BANKS = 4
-ON_VECTOR = ()
+ON_VECTOR = (3,)
 LOG_PARTS = 2
 ON_POOL = (0,)
 LAST_POOL = ()
@@ -207,7 +207,7 @@ def tile_diffscm_pb_t_kernel(
                 )
 
         def by_vector(k):
-            return ON_VECTOR if k < QUADS - 2 else ()
+            return ON_VECTOR if k < QUADS - 2 and k % 2 == 1 else ()
 
         def by_pool(k):
             return ON_POOL if k < QUADS - 2 else LAST_POOL

@@ -277,24 +277,23 @@ def tile_diffscm_pb_t_kernel(
         gates(1)
         log(0)
         log(1)
-        nc.vector.tensor_copy(out=t_f32[:], in_=t_bf[:])
-        nc.vector.tensor_scalar(out=one_minus_t[:], in0=t_bf[:], scalar1=-1.0, scalar2=1.0, op0=ALU.mult, op1=ALU.add)
-        keep_share(0)
-        keep_share(1)
         for k in range(3, HEAD_QUADS):
             turn_quad(k)
+        quantise(HEAD_QUADS - 1)
+        nc.vector.tensor_copy(out=t_f32[:], in_=t_bf[:])
+        nc.vector.tensor_scalar(out=one_minus_t[:], in0=t_bf[:], scalar1=-1.0, scalar2=1.0, op0=ALU.mult, op1=ALU.add)
 
         for a in range(0, QUADS, 2):
             b = a + 1
             more = valid(a + 2)
+            keep_share(a)
+            keep_share(b)
             for j in range(BLOCKS):
                 if j not in by_vector(a):
                     mean(a, j)
             for k in (a, b):
                 for j in range(BLOCKS):
                     clamp(k, j)
-            if a == 0:
-                quantise(HEAD_QUADS - 1)
             for k in (a, b):
                 for j in range(BLOCKS):
                     if k == b and j not in by_vector(k):
@@ -304,9 +303,6 @@ def tile_diffscm_pb_t_kernel(
                     for j in (2 * half, 2 * half + 1):
                         if j not in by_vector(k) and j in by_pool(k):
                             pool_add(k, j)
-            for k in (a + 2, a + 3):
-                if valid(k):
-                    keep_share(k)
             if more:
                 nc.scalar.activation(out=warm[:, 1:2], in_=warm[:, 0:1], func=ACT.Sigmoid)
             for k in (a, b):

@@ -289,11 +289,12 @@ def tile_diffscm_pb_t_kernel(
             keep_share(a)
             keep_share(b)
             for j in range(BLOCKS):
+                clamp(a, j)
+            for j in range(BLOCKS):
                 if j not in by_vector(a):
                     mean(a, j)
-            for k in (a, b):
-                for j in range(BLOCKS):
-                    clamp(k, j)
+            for j in range(BLOCKS):
+                clamp(b, j)
             for k in (a, b):
                 for j in range(BLOCKS):
                     if k == b and j not in by_vector(k):

@@ -28,7 +28,7 @@ V_BANKS = 4
 ON_VECTOR = (3,)
 LOG_PARTS = 2
 ON_POOL = (0,)
-LAST_POOL = ()
+LAST_POOL = (0,)
 TINY = 2.0 ** -63
 
 FLOPS = 2 * 2 * ROWS * D * D

from contextlib import ExitStack

import concourse.mybir as mybir
from concourse.masks import make_identity

F32 = mybir.dt.float32
BF16 = mybir.dt.bfloat16
I32 = mybir.dt.int32
U32 = mybir.dt.uint32
U8 = mybir.dt.uint8
FP8X4 = mybir.dt.float8_e4m3fn_x4
FP4X4 = mybir.dt.float4_e2m1fn_x4
ALU = mybir.AluOpType
ACT = mybir.ActivationFunctionType

P = 128
ROWS = 4096
D = 512
TILES = ROWS // P
QUAD = 4
QUADS = TILES // QUAD
BLOCKS = D // P
LOAD = 8
WARM_FIRST = 6
HEAD_QUADS = 5
S_BANKS = 4
V_BANKS = 4
ON_VECTOR = (3,)
LOG_PARTS = 2
ON_POOL = (0,)
LAST_POOL = (0,)
TINY = 2.0 ** -63

FLOPS = 2 * 2 * ROWS * D * D


def load_fp4_weight(nc, pool, words, scales, name):
    w_words = pool.tile([P, 2 * D], U8, name=name + "_words", align_bytes=64)
    nc.sync.dma_start(out=w_words[:].bitcast(I32), in_=words[0].bitcast(I32))
    w_plane = pool.tile([P, D], U8, name=name + "_plane", align_bytes=64)
    nc.vector.memset(w_plane[:].bitcast(I32), 0)
    for quadrant in range(4):
        nc.sync.dma_start(
            out=w_plane[32 * quadrant : 32 * quadrant + 4, :].bitcast(I32),
            in_=scales[0, 4 * quadrant : 4 * quadrant + 4, :].bitcast(I32),
        )
    return w_words, w_plane


def tile_diffscm_pb_t_kernel(
    tc, xt, eps, x, t_rand, Wm_words, Wm_scales, bm, Wv_words, Wv_scales, bv, out
):
    nc = tc.nc
    xt_rows = xt.rearrange("(p i) k -> p i k", i=TILES)
    eps_rows = eps.rearrange("(p i) n -> p i n", i=TILES)
    x_rows = x.rearrange("(p i) n -> p i n", i=TILES)
    out_rows = out.rearrange("(p i) n -> p i n", i=TILES)

    with ExitStack() as ctx:
        keep = ctx.enter_context(tc.tile_pool(name="keep", bufs=1))
        flow = ctx.enter_context(tc.tile_pool(name="flow", bufs=2))
        psum = ctx.enter_context(tc.psum_pool(name="psum", bufs=1))
        ctx.enter_context(tc.manual_schedule())

        xt_sb = keep.tile([P, TILES, D], BF16, name="xt_sb")
        eps_sb = keep.tile([P, TILES, D], BF16, name="eps_sb")
        x_sb = keep.tile([P, TILES, D], BF16, name="x_sb")

        def load(dst, src, k):
            rows = slice(k * QUAD, (k + 1) * QUAD)
            nc.sync.dma_start(out=dst[:, rows, :], in_=src[:, rows, :])

        nc.sync.dma_start(out=xt_sb[:, 0:2, :], in_=xt_rows[:, 0:2, :])
        nc.sync.dma_start(out=xt_sb[:, 2:QUAD, :], in_=xt_rows[:, 2:QUAD, :])
        load(xt_sb, xt_rows, 1)
        wv_words, wv_plane = load_fp4_weight(nc, keep, Wv_words, Wv_scales, "wv")
        bias_rows = keep.tile([P, P], BF16, name="bias_rows")
        nc.vector.memset(bias_rows[:], 0.0)
        nc.scalar.dma_start(out=bias_rows[0:BLOCKS, :], in_=bv.rearrange("(j p) -> j p", p=P))
        nc.scalar.dma_start(out=bias_rows[BLOCKS : 2 * BLOCKS, :], in_=bm.rearrange("(j p) -> j p", p=P))
        t_bf = keep.tile([P, TILES], BF16, name="t_bf")
        nc.scalar.dma_start(out=t_bf[:], in_=t_rand.rearrange("(p i) o -> p (i o)", i=TILES))
        for k in range(2, HEAD_QUADS):
            load(xt_sb, xt_rows, k)
        wm_words, wm_plane = load_fp4_weight(nc, keep, Wm_words, Wm_scales, "wm")
        for k in range(QUADS):
            load(eps_sb, eps_rows, k)
            load(x_sb, x_rows, k)
            if k == 1:
                for later in range(HEAD_QUADS, QUADS):
                    load(xt_sb, xt_rows, later)

        ident = keep.tile([P, P], F32, name="ident")
        make_identity(nc, ident[:])
        ident_bf = keep.tile([P, P], BF16, name="ident_bf")
        make_identity(nc, ident_bf[:])
        t_f32 = keep.tile([P, TILES], F32, name="t_f32")
        one_minus_t = keep.tile([P, TILES], F32, name="one_minus_t")
        bv_cols = keep.tile([P, BLOCKS], F32, name="bv_cols")
        bm_cols = keep.tile([P, BLOCKS], F32, name="bm_cols")
        grouped_of = {}
        turned_of = {}
        codes_of = {}
        spread_of = {}
        mean_of = {}
        kept_of = {}

        def turn(k, i, by_scalar):
            if i == 0:
                grouped_of[k] = flow.tile([P, QUAD * P * 4], BF16, name="grouped", bufs=3, align_bytes=64)
            if i % 2 == 0:
                if by_scalar:
                    turned_of[k] = psum.tile([P, 2, 2, P], F32, name="turned_s", tag="for_scalar", bufs=S_BANKS)
                else:
                    turned_of[k] = psum.tile([P, 2, 2, P], F32, name="turned", tag="for_vector", bufs=V_BANKS)
            words = xt_sb[:, k * QUAD + i, :].bitcast(F32)
            for h in range(2):
                nc.tensor.transpose(turned_of[k][:, i % 2, h, :], words[:, h : D // 2 : 2], ident[:])
            if i % 2 == 1:
                grouped_words = grouped_of[k][:].bitcast(F32).rearrange("p (i r h) -> p i r h", i=QUAD, r=P, h=2)
                copy = nc.scalar.copy if by_scalar else nc.vector.tensor_copy
                copy(
                    out=grouped_words[:, i - 1 : i + 1, :, :],
                    in_=turned_of[k][:].rearrange("p i h r -> p i r h"),
                )

        def quantise(k):
            codes = flow.tile([P, QUAD * P], U32, name="codes", bufs=QUADS, align_bytes=64)
            planes = flow.tile([P, QUAD * P], U8, name="planes", bufs=QUADS, align_bytes=64)
            nc.vector.quantize_mx(out=codes[:].bitcast(FP8X4), scales=planes[:], in_=grouped_of[k][:])
            codes_of[k] = (codes, planes)

        def head(acc, w_words, w_plane, j, k):
            codes, planes = codes_of[k]
            nc.tensor.matmul_mx(
                out=acc[:],
                lhsT=w_words[:, 2 * P * j : 2 * P * (j + 1)].bitcast(FP4X4),
                lhsT_scale=w_plane[:, P * j : P * (j + 1)],
                rhs=codes[:].bitcast(FP8X4),
                rhs_scale=planes[:],
                start=True,
                stop=True,
            )

        def gate(k, j):
            if j == 0:
                spread_of[k] = flow.tile([P, BLOCKS, QUAD * P], F32, name="spread", bufs=4)
            acc = psum.tile([P, QUAD * P], F32, name="acc_gate", tag="for_scalar", bufs=S_BANKS)
            head(acc, wv_words, wv_plane, j, k)
            nc.scalar.activation(
                out=spread_of[k][:, j, :], in_=acc[:], func=ACT.Sigmoid, bias=bv_cols[:, j : j + 1]
            )

        def log(k):
            for half in range(LOG_PARTS):
                blocks = slice(half * BLOCKS // LOG_PARTS, (half + 1) * BLOCKS // LOG_PARTS)
                part = spread_of[k][:, blocks, :]
                nc.scalar.activation(out=part, in_=part, func=ACT.Ln, bias=TINY)

        def mean(k, j):
            if j == 0:
                mean_of[k] = flow.tile([P, BLOCKS, QUAD * P], F32, name="mean", bufs=3)
            acc = psum.tile([P, QUAD * P], F32, name="acc_mean", tag="for_scalar", bufs=S_BANKS)
            head(acc, wm_words, wm_plane, j, k)
            nc.scalar.activation(
                out=mean_of[k][:, j, :], in_=acc[:], func=ACT.Identity, bias=bm_cols[:, j : j + 1]
            )

        def clamp(k, j):
            acc = psum.tile([P, QUAD * P], F32, name="acc_clamp", tag="for_vector", bufs=V_BANKS)
            head(acc, wv_words, wv_plane, j, k)
            part = spread_of[k][:, j, :]
            nc.vector.scalar_tensor_tensor(
                out=part, in0=acc[:], scalar=bv_cols[:, j : j + 1], in1=part, op0=ALU.add, op1=ALU.subtract
            )

        def noise(k, half):
            eps_t = psum.tile([P, 2, QUAD * P], BF16, name="eps_t", tag="for_vector", bufs=V_BANKS)
            for h in range(2):
                j = 2 * half + h
                for i in range(QUAD):
                    nc.tensor.transpose(
                        eps_t[:, h, i * P : (i + 1) * P], eps_sb[:, k * QUAD + i, j * P : (j + 1) * P], ident_bf[:]
                    )
            part = spread_of[k][:, 2 * half : 2 * half + 2, :]
            nc.vector.scalar_tensor_tensor(out=part, in0=part, scalar=0.0, in1=eps_t[:], op0=ALU.max, op1=ALU.mult)

        def sample(k, j):
            acc = psum.tile([P, QUAD * P], F32, name="acc_sample", tag="for_vector", bufs=V_BANKS)
            head(acc, wm_words, wm_plane, j, k)
            part = spread_of[k][:, j, :]
            nc.vector.scalar_tensor_tensor(
                out=part, in0=acc[:], scalar=bm_cols[:, j : j + 1], in1=part, op0=ALU.add, op1=ALU.add
            )

        def pool_add(k, j):
            part = spread_of[k][:, j, :]
            nc.gpsimd.tensor_tensor(out=part, in0=part, in1=mean_of[k][:, j, :], op=ALU.add)

        def keep_share(k):
            kept_of[k] = flow.tile([P, QUAD, D], F32, name="kept", bufs=4)
            for i in range(QUAD):
                row = k * QUAD + i
                nc.gpsimd.tensor_scalar(
                    out=kept_of[k][:, i, :], in0=x_sb[:, row, :], scalar1=one_minus_t[:, row : row + 1], scalar2=0.0,
                    op0=ALU.mult, op1=ALU.add,
                )

        def by_vector(k):
            return ON_VECTOR if k < QUADS - 2 and k % 2 == 1 else ()

        def by_pool(k):
            return ON_POOL if k < QUADS - 2 else LAST_POOL

        def blend(k, i):
            back = psum.tile([P, D], F32, name="back", tag="for_vector", bufs=V_BANKS)
            rows = slice(i * P, (i + 1) * P)
            for j in range(BLOCKS):
                cols = slice(j * P, (j + 1) * P)
                if j not in by_vector(k) and j not in by_pool(k):
                    nc.tensor.matmul(
                        out=back[:, cols], lhsT=mean_of[k][:, j, rows], rhs=ident[:], is_transpose=True,
                        start=True, stop=False,
                    )
                nc.tensor.matmul(
                    out=back[:, cols], lhsT=spread_of[k][:, j, rows], rhs=ident[:], is_transpose=True,
                    start=j in by_vector(k) or j in by_pool(k), stop=True,
                )
            row = k * QUAD + i
            nc.vector.scalar_tensor_tensor(
                out=kept_of[k][:, i, :], in0=back[:], scalar=t_f32[:, row : row + 1], in1=kept_of[k][:, i, :],
                op0=ALU.mult, op1=ALU.add,
            )

        zeros = keep.tile([P, D], BF16, name="zeros")
        nc.vector.memset(zeros[:], 0.0)

        def idle_work(n):
            for spare_pass in range(n):
                spare = psum.tile([P, D], F32, name="spare", tag="for_scalar", bufs=S_BANKS)
                nc.tensor.matmul(out=spare[:], lhsT=zeros[:, 0:P], rhs=zeros[:], start=True, stop=True)

        idle_work(WARM_FIRST)
        warm = keep.tile([P, 2], F32, name="warm")
        nc.vector.memset(warm[:], 0.0)
        nc.scalar.activation(out=warm[:, 1:2], in_=warm[:, 0:1], func=ACT.Sigmoid)

        def valid(k):
            return 0 <= k < QUADS

        def finish(k):
            for i in range(QUAD):
                blend(k, i)
                nc.sync.dma_start(out=out_rows[:, k * QUAD + i, :], in_=kept_of[k][:, i, :])


        def turn_quad(k):
            for i in range(QUAD):
                turn(k, i, False)
                if i == 1 and valid(k - 1) and k - 1 not in codes_of:
                    quantise(k - 1)

        def gates(k):
            for j in range(BLOCKS):
                gate(k, j)

        turn_quad(0)
        bias_cols = psum.tile([P, P], BF16, name="bias_cols", tag="for_vector", bufs=V_BANKS)
        nc.tensor.transpose(bias_cols[:], bias_rows[:], ident_bf[:])
        nc.vector.tensor_copy(out=bv_cols[:], in_=bias_cols[:, 0:BLOCKS])
        nc.vector.tensor_copy(out=bm_cols[:], in_=bias_cols[:, BLOCKS : 2 * BLOCKS])
        quantise(0)
        turn_quad(1)
        quantise(1)
        gates(0)
        turn_quad(2)
        gates(1)
        log(0)
        log(1)
        for k in range(3, HEAD_QUADS):
            turn_quad(k)
        quantise(HEAD_QUADS - 1)
        nc.vector.tensor_copy(out=t_f32[:], in_=t_bf[:])
        nc.vector.tensor_scalar(out=one_minus_t[:], in0=t_bf[:], scalar1=-1.0, scalar2=1.0, op0=ALU.mult, op1=ALU.add)

        for a in range(0, QUADS, 2):
            b = a + 1
            more = valid(a + 2)
            keep_share(a)
            keep_share(b)
            for j in range(BLOCKS):
                clamp(a, j)
            for j in range(BLOCKS):
                if j not in by_vector(a):
                    mean(a, j)
            for j in range(BLOCKS):
                clamp(b, j)
            for k in (a, b):
                for j in range(BLOCKS):
                    if k == b and j not in by_vector(k):
                        mean(k, j)
                for half in range(2):
                    noise(k, half)
                    for j in (2 * half, 2 * half + 1):
                        if j not in by_vector(k) and j in by_pool(k):
                            pool_add(k, j)
            if more:
                nc.scalar.activation(out=warm[:, 1:2], in_=warm[:, 0:1], func=ACT.Sigmoid)
            for k in (a, b):
                for j in by_vector(k):
                    sample(k, j)
            if more:
                gates(a + 2)
            finish(a)
            if more:
                gates(a + 3)
                log(a + 2)
                log(a + 3)
            finish(b)
            for k in (HEAD_QUADS + a, HEAD_QUADS + a + 1):
                if valid(k):
                    turn_quad(k)
                    if k == QUADS - 1:
                        quantise(k)
